import numpy as np
import ml_dtypes


def mxq(x, axis, fmt="e4m3"):
    dtype, down = {"e4m3": (ml_dtypes.float8_e4m3fn, 7), "e5m2": (ml_dtypes.float8_e5m2, 14)}[fmt]
    v = np.moveaxis(np.asarray(x, np.float32).astype(ml_dtypes.bfloat16).astype(np.float64), axis, -1)
    blocks = v.reshape(v.shape[:-1] + (-1, 32))
    amax = np.abs(blocks).max(-1, keepdims=True)
    byte = np.maximum(np.where(amax > 0, np.frexp(amax)[1] - 1 + 127, 0) - down, 1)
    scale = np.exp2(byte - 127.0)
    codes = (blocks / scale).astype(np.float32).astype(dtype).astype(np.float64)
    return np.moveaxis((codes * scale).reshape(v.shape), -1, axis)


WIDE = False


def mx_kscale(k):
    if not WIDE:
        return np.ones(k)
    levels = np.array([10, -10, 5, -5, 0])
    a = np.random.permutation(np.resize(levels, k // 512 * 4)).reshape(k // 512, 4)
    idx = np.arange(k)
    return np.exp2(a[idx // 512, idx % 128 // 32])


BF16 = ml_dtypes.bfloat16


def bf(x):
    return np.asarray(x, np.float32).astype(BF16)


def f64(x):
    return np.asarray(x).astype(np.float64)


E2M1 = np.array([0.0, 0.5, 1.0, 1.5, 2.0, 3.0, 4.0, 6.0, -0.0, -0.5, -1.0, -1.5, -2.0, -3.0, -4.0, -6.0])


def pack_weight(w, fmt):
    k, n = w.shape
    w = f64(bf(w)).reshape(k // 32, 32, n)
    amax = np.abs(w).max(1)
    if fmt == "e4m3":
        byte = np.frexp(amax)[1] - 1 + 127 - 7
    else:
        mant, ex = np.frexp(amax / 6.0)
        byte = np.where(mant > 0.5, ex, ex - 1) + 127
    byte = np.clip(np.where(amax > 0, byte, 1), 1, 254)
    scaled = (w * np.exp2(127.0 - byte)[:, None, :]).reshape(k, n).astype(np.float32)
    by_word = np.ascontiguousarray(scaled.reshape(k // 512, 128, 4, n).transpose(0, 1, 3, 2))
    if fmt == "e4m3":
        words = by_word.astype(ml_dtypes.float8_e4m3fn).view(np.uint8)
    else:
        c = by_word.astype(ml_dtypes.float4_e2m1fn).view(np.uint8) & 0xF
        words = c[..., 0::2] | (c[..., 1::2] << 4)
    return np.ascontiguousarray(words), np.ascontiguousarray(byte.astype(np.uint8).reshape(k // 512, 16, n))


def unpack_weight(words, scales, fmt):
    g, p, n, _ = words.shape
    if fmt == "e4m3":
        vals = np.ascontiguousarray(words).view(ml_dtypes.float8_e4m3fn).astype(np.float64)
    else:
        nib = np.empty((g, p, n, 4), np.uint8)
        nib[..., 0::2] = words & 0xF
        nib[..., 1::2] = words >> 4
        vals = E2M1[nib]
    vals = vals * np.repeat(np.exp2(scales.astype(np.float64) - 127.0), 8, axis=1)[..., None]
    return vals.transpose(0, 1, 3, 2).reshape(g * 512, n)

def pack4(w):
    words, scales = pack_weight(w, "e2m1")
    return words.reshape(words.shape[0], 128, -1), scales


def unpack4(words, scales):
    return unpack_weight(words.reshape(words.shape[0], 128, -1, 2), scales, "e2m1")


N, LMAX, CIN, COUT = 128, 3, 1024, 1024
NL = LMAX + 1
NM = NL * NL


def setup_inputs():
    s = mx_kscale(CIN)
    x = bf(np.random.standard_normal((N, NM, CIN)) * s)
    stack = np.random.standard_normal((NL, CIN, COUT)) / np.sqrt(CIN) / s[:, None]
    words, scales = pack4(stack.reshape(-1, COUT))
    path_weights = bf(1.0 + 0.3 * np.random.standard_normal(NL))
    return {"x": x,
            "weights_words": words,
            "weights_scales": scales,
            "path_weights": path_weights}


def reference(x, weights_words, weights_scales, path_weights):
    x, path_weights = f64(x), f64(path_weights)
    weights = unpack4(weights_words, weights_scales).reshape(NL, CIN, COUT)
    blocks = []
    for l in range(LMAX + 1):
        start = l * l
        end = start + (2 * l + 1)
        blk = mxq(x[:, start:end, :], 2, "e4m3") @ weights[l]
        blocks.append(path_weights[l] * blk)
    return np.concatenate(blocks, axis=1)

@@ -1,0 +1,141 @@
+from contextlib import ExitStack
+
+import concourse.masks as masks
+import concourse.mybir as mybir
+
+F32 = mybir.dt.float32
+BF16 = mybir.dt.bfloat16
+I32 = mybir.dt.int32
+U32 = mybir.dt.uint32
+U8 = mybir.dt.uint8
+FP8X4 = mybir.dt.float8_e4m3fn_x4
+FP4X4 = mybir.dt.float4_e2m1fn_x4
+
+P = 128
+ROWS = 16
+DEGREES = 4
+CIN = 1024
+COUT = 1024
+K_PASS = 4 * P
+PASSES = CIN // K_PASS
+N_TILE = 512
+HALVES = COUT // N_TILE
+WORDS = 2
+BUNCH = 4
+STORE_ROWS = 2
+
+DEGREE_OF_ROW = [l for l in range(DEGREES) for i in range(2 * l + 1)]
+
+FLOPS = 2 * P * ROWS * CIN * COUT
+
+
+def tile_linear_pa_e_kernel(tc, x, weights_words, weights_scales, path_weights, out):
+    nc = tc.nc
+    with ExitStack() as ctx:
+        keep = ctx.enter_context(tc.tile_pool(name="keep", bufs=1))
+        xt_pool = ctx.enter_context(tc.psum_pool(name="xt_pool", bufs=BUNCH))
+        acc_pool = ctx.enter_context(tc.psum_pool(name="acc_pool", bufs=8 - BUNCH))
+        ctx.enter_context(tc.manual_schedule())
+
+        x_sb = keep.tile([P, ROWS, CIN], BF16)
+        w_words = keep.tile([P, DEGREES * PASSES, 2 * COUT], U8, align_bytes=64)
+        w_planes = keep.tile([P, DEGREES * PASSES, COUT], U8, align_bytes=64)
+        grouped = keep.tile([P, ROWS, CIN], BF16, align_bytes=64)
+        x_codes = keep.tile([P, ROWS, PASSES, P], U32, align_bytes=64)
+        x_planes = keep.tile([P, ROWS, PASSES, P], U8, align_bytes=64)
+        out_sb = keep.tile([P, ROWS, COUT], F32)
+        ident = keep.tile([P, P], F32)
+        factor_bf = keep.tile([P, DEGREES], BF16)
+        factor = keep.tile([P, DEGREES], F32)
+
+        masks.make_identity(nc, ident[:])
+
+        nc.scalar.dma_start(out=factor_bf[:], in_=path_weights.partition_broadcast(P))
+
+        words_i32 = weights_words.bitcast(I32)
+        scales_i32 = weights_scales.bitcast(I32)
+
+        def load_x(first_row, n_rows):
+            rows = slice(first_row, first_row + n_rows)
+            nc.sync.dma_start(out=x_sb[:, rows, :], in_=x[:, rows, :])
+
+        def load_weight(l):
+            groups = slice(PASSES * l, PASSES * (l + 1))
+            nc.vector.memset(w_planes[:, groups, :].bitcast(I32), 0)
+            for r in range(4):
+                nc.sync.dma_start(
+                    out=w_planes[r:P:32, groups, :].bitcast(I32),
+                    in_=scales_i32[groups, r:16:4, :].rearrange("g q n -> q g n"),
+                )
+            nc.sync.dma_start(
+                out=w_words[:, groups, :].bitcast(I32),
+                in_=words_i32[groups, :, :].rearrange("g p w -> p g w"),
+            )
+
+        def transpose_and_quantise(m):
+            x_words = x_sb[:, m, :].bitcast(F32)
+            xt = xt_pool.tile([P, PASSES, WORDS, P], F32)
+            for g in range(PASSES):
+                for u in range(WORDS):
+                    columns = slice(WORDS * P * g + u, WORDS * P * (g + 1), WORDS)
+                    nc.tensor.transpose(xt[:, g, u, :], x_words[:, columns], ident[:])
+            nc.vector.tensor_copy(
+                out=grouped[:, m, :].bitcast(F32).rearrange("p (g n u) -> p g n u", g=PASSES, u=WORDS),
+                in_=xt[:].rearrange("p g u n -> p g n u"),
+            )
+            nc.vector.quantize_mx(
+                out=x_codes[:, m, :, :].rearrange("p g n -> p (g n)").bitcast(FP8X4),
+                scales=x_planes[:, m, :, :].rearrange("p g n -> p (g n)"),
+                in_=grouped[:, m, :],
+            )
+
+        def multiply(m):
+            l = DEGREE_OF_ROW[m]
+            for h in range(HALVES):
+                acc = acc_pool.tile([P, N_TILE], F32)
+                for g in range(PASSES):
+                    nc.tensor.matmul_mx(
+                        out=acc[:],
+                        lhsT=x_codes[:, m, g, :].bitcast(FP8X4),
+                        lhsT_scale=x_planes[:, m, g, :],
+                        rhs=w_words[:, PASSES * l + g, 2 * N_TILE * h : 2 * N_TILE * (h + 1)].bitcast(FP4X4),
+                        rhs_scale=w_planes[:, PASSES * l + g, N_TILE * h : N_TILE * (h + 1)],
+                        start=(g == 0),
+                        stop=(g == PASSES - 1),
+                    )
+                result = out_sb[:, m, N_TILE * h : N_TILE * (h + 1)]
+                if m % 2 == 0 and h == HALVES - 1:
+                    nc.vector.tensor_scalar_mul(out=result, in0=acc[:], scalar1=factor[:, l : l + 1])
+                else:
+                    nc.scalar.activation(
+                        out=result,
+                        in_=acc[:],
+                        func=mybir.ActivationFunctionType.Copy,
+                        scale=factor[:, l : l + 1],
+                    )
+            if m % STORE_ROWS == 0:
+                rows = slice(m, m + STORE_ROWS)
+                nc.sync.dma_start(out=out[:, rows, :], in_=out_sb[:, rows, :])
+
+        load_x(ROWS - BUNCH // 2, BUNCH // 2)
+        load_x(ROWS - BUNCH, BUNCH // 2)
+        load_weight(3)
+        load_x(ROWS - 2 * BUNCH, BUNCH)
+        load_weight(2)
+        load_x(ROWS - 3 * BUNCH, BUNCH)
+        load_weight(1)
+        load_weight(0)
+        load_x(ROWS - 4 * BUNCH, BUNCH)
+        nc.vector.tensor_copy(out=factor[:], in_=factor_bf[:])
+
+        bunches = [list(range(top - 1, top - 1 - BUNCH, -1)) for top in range(ROWS, 0, -BUNCH)]
+        for m in bunches[0]:
+            transpose_and_quantise(m)
+        for b in range(len(bunches)):
+            for m in bunches[b][: BUNCH // 2]:
+                multiply(m)
+            if b + 1 < len(bunches):
+                for m in bunches[b + 1]:
+                    transpose_and_quantise(m)
+            for m in bunches[b][BUNCH // 2 :]:
+                multiply(m)

@@ -22,6 +22,7 @@ N_TILE = 512
 HALVES = COUT // N_TILE
 WORDS = 2
 BUNCH = 4
+HEAD = 2
 STORE_ROWS = 2
 
 DEGREE_OF_ROW = [l for l in range(DEGREES) for i in range(2 * l + 1)]
@@ -38,8 +39,12 @@ def tile_linear_pa_e_kernel(tc, x, weights_words, weights_scales, path_weights, 
         ctx.enter_context(tc.manual_schedule())
 
         x_sb = keep.tile([P, ROWS, CIN], BF16)
-        w_words = keep.tile([P, DEGREES * PASSES, 2 * COUT], U8, align_bytes=64)
-        w_planes = keep.tile([P, DEGREES * PASSES, COUT], U8, align_bytes=64)
+        w_words = [
+            keep.tile([P, PASSES, 2 * COUT], U8, align_bytes=64, name="w_words%d" % l) for l in range(DEGREES)
+        ]
+        w_planes = [
+            keep.tile([P, PASSES, COUT], U8, align_bytes=64, name="w_planes%d" % l) for l in range(DEGREES)
+        ]
         grouped = keep.tile([P, ROWS, CIN], BF16, align_bytes=64)
         x_codes = keep.tile([P, ROWS, PASSES, P], U32, align_bytes=64)
         x_planes = keep.tile([P, ROWS, PASSES, P], U8, align_bytes=64)
@@ -61,14 +66,14 @@ def tile_linear_pa_e_kernel(tc, x, weights_words, weights_scales, path_weights, 
 
         def load_weight(l):
             groups = slice(PASSES * l, PASSES * (l + 1))
-            nc.vector.memset(w_planes[:, groups, :].bitcast(I32), 0)
+            nc.vector.memset(w_planes[l][:].bitcast(I32), 0)
             for r in range(4):
                 nc.sync.dma_start(
-                    out=w_planes[r:P:32, groups, :].bitcast(I32),
+                    out=w_planes[l][r:P:32, :, :].bitcast(I32),
                     in_=scales_i32[groups, r:16:4, :].rearrange("g q n -> q g n"),
                 )
             nc.sync.dma_start(
-                out=w_words[:, groups, :].bitcast(I32),
+                out=w_words[l][:].bitcast(I32),
                 in_=words_i32[groups, :, :].rearrange("g p w -> p g w"),
             )
 
@@ -98,8 +103,8 @@ def tile_linear_pa_e_kernel(tc, x, weights_words, weights_scales, path_weights, 
                         out=acc[:],
                         lhsT=x_codes[:, m, g, :].bitcast(FP8X4),
                         lhsT_scale=x_planes[:, m, g, :],
-                        rhs=w_words[:, PASSES * l + g, 2 * N_TILE * h : 2 * N_TILE * (h + 1)].bitcast(FP4X4),
-                        rhs_scale=w_planes[:, PASSES * l + g, N_TILE * h : N_TILE * (h + 1)],
+                        rhs=w_words[l][:, g, 2 * N_TILE * h : 2 * N_TILE * (h + 1)].bitcast(FP4X4),
+                        rhs_scale=w_planes[l][:, g, N_TILE * h : N_TILE * (h + 1)],
                         start=(g == 0),
                         stop=(g == PASSES - 1),
                     )
@@ -113,29 +118,32 @@ def tile_linear_pa_e_kernel(tc, x, weights_words, weights_scales, path_weights, 
                         func=mybir.ActivationFunctionType.Copy,
                         scale=factor[:, l : l + 1],
                     )
-            if m % STORE_ROWS == 0:
+                if m < STORE_ROWS:
+                    nc.sync.dma_start(out=out[:, m, N_TILE * h : N_TILE * (h + 1)], in_=result)
+            if m >= STORE_ROWS and m % STORE_ROWS == 0:
                 rows = slice(m, m + STORE_ROWS)
                 nc.sync.dma_start(out=out[:, rows, :], in_=out_sb[:, rows, :])
 
-        load_x(ROWS - BUNCH // 2, BUNCH // 2)
-        load_x(ROWS - BUNCH, BUNCH // 2)
-        load_weight(3)
-        load_x(ROWS - 2 * BUNCH, BUNCH)
-        load_weight(2)
-        load_x(ROWS - 3 * BUNCH, BUNCH)
-        load_weight(1)
-        load_weight(0)
-        load_x(ROWS - 4 * BUNCH, BUNCH)
+        order = list(range(ROWS - 1, -1, -1))
+        bunches = [order[:HEAD]] + [order[i : i + BUNCH] for i in range(HEAD, ROWS, BUNCH)]
+
+        loaded = set()
+        for rows in bunches:
+            load_x(rows[-1], len(rows))
+            for m in rows:
+                if DEGREE_OF_ROW[m] not in loaded:
+                    loaded.add(DEGREE_OF_ROW[m])
+                    load_weight(DEGREE_OF_ROW[m])
         nc.vector.tensor_copy(out=factor[:], in_=factor_bf[:])
 
-        bunches = [list(range(top - 1, top - 1 - BUNCH, -1)) for top in range(ROWS, 0, -BUNCH)]
         for m in bunches[0]:
             transpose_and_quantise(m)
         for b in range(len(bunches)):
-            for m in bunches[b][: BUNCH // 2]:
+            half = len(bunches[b]) // 2
+            for m in bunches[b][:half]:
                 multiply(m)
             if b + 1 < len(bunches):
                 for m in bunches[b + 1]:
                     transpose_and_quantise(m)
-            for m in bunches[b][BUNCH // 2 :]:
+            for m in bunches[b][half:]:
                 multiply(m)

@@ -39,6 +39,7 @@ def tile_linear_pa_e_kernel(tc, x, weights_words, weights_scales, path_weights, 
         ctx.enter_context(tc.manual_schedule())
 
         x_sb = keep.tile([P, ROWS, CIN], BF16)
+        x_sorted = keep.tile([P, ROWS, CIN], BF16)
         w_words = [
             keep.tile([P, PASSES, 2 * COUT], U8, align_bytes=64, name="w_words%d" % l) for l in range(DEGREES)
         ]
@@ -77,22 +78,34 @@ def tile_linear_pa_e_kernel(tc, x, weights_words, weights_scales, path_weights, 
                 in_=words_i32[groups, :, :].rearrange("g p w -> p g w"),
             )
 
-        def transpose_and_quantise(m):
-            x_words = x_sb[:, m, :].bitcast(F32)
-            xt = xt_pool.tile([P, PASSES, WORDS, P], F32)
-            for g in range(PASSES):
-                for u in range(WORDS):
-                    columns = slice(WORDS * P * g + u, WORDS * P * (g + 1), WORDS)
-                    nc.tensor.transpose(xt[:, g, u, :], x_words[:, columns], ident[:])
+        def sort_words(rows):
+            block = slice(rows[-1], rows[0] + 1)
             nc.vector.tensor_copy(
-                out=grouped[:, m, :].bitcast(F32).rearrange("p (g n u) -> p g n u", g=PASSES, u=WORDS),
-                in_=xt[:].rearrange("p g u n -> p g n u"),
+                out=x_sorted[:, block, :].bitcast(F32).rearrange("p m (g u q) -> p (m g) u q", g=PASSES, u=WORDS),
+                in_=x_sb[:, block, :].bitcast(F32).rearrange("p m (g q u) -> p (m g) u q", g=PASSES, u=WORDS),
             )
+
+        def quantise(m):
             nc.vector.quantize_mx(
                 out=x_codes[:, m, :, :].rearrange("p g n -> p (g n)").bitcast(FP8X4),
                 scales=x_planes[:, m, :, :].rearrange("p g n -> p (g n)"),
                 in_=grouped[:, m, :],
             )
+
+        def transpose_and_quantise(rows):
+            for i in range(len(rows)):
+                m = rows[i]
+                x_words = x_sorted[:, m, :].bitcast(F32)
+                xt = xt_pool.tile([P, PASSES * WORDS, P], F32)
+                for j in range(PASSES * WORDS):
+                    nc.tensor.transpose(xt[:, j, :], x_words[:, P * j : P * (j + 1)], ident[:])
+                nc.vector.tensor_copy(
+                    out=grouped[:, m, :].bitcast(F32).rearrange("p (g n u) -> p g n u", g=PASSES, u=WORDS),
+                    in_=xt[:].rearrange("p (g u) n -> p g n u", u=WORDS),
+                )
+                if i > 0:
+                    quantise(rows[i - 1])
+            quantise(rows[-1])
 
         def multiply(m):
             l = DEGREE_OF_ROW[m]
@@ -109,15 +122,12 @@ def tile_linear_pa_e_kernel(tc, x, weights_words, weights_scales, path_weights, 
                         stop=(g == PASSES - 1),
                     )
                 result = out_sb[:, m, N_TILE * h : N_TILE * (h + 1)]
-                if m % 2 == 0 and h == HALVES - 1:
-                    nc.vector.tensor_scalar_mul(out=result, in0=acc[:], scalar1=factor[:, l : l + 1])
-                else:
-                    nc.scalar.activation(
-                        out=result,
-                        in_=acc[:],
-                        func=mybir.ActivationFunctionType.Copy,
-                        scale=factor[:, l : l + 1],
-                    )
+                nc.scalar.activation(
+                    out=result,
+                    in_=acc[:],
+                    func=mybir.ActivationFunctionType.Copy,
+                    scale=factor[:, l : l + 1],
+                )
                 if m < STORE_ROWS:
                     nc.sync.dma_start(out=out[:, m, N_TILE * h : N_TILE * (h + 1)], in_=result)
             if m >= STORE_ROWS and m % STORE_ROWS == 0:
@@ -137,13 +147,17 @@ def tile_linear_pa_e_kernel(tc, x, weights_words, weights_scales, path_weights, 
         nc.vector.tensor_copy(out=factor[:], in_=factor_bf[:])
 
         for m in bunches[0]:
-            transpose_and_quantise(m)
+            sort_words([m])
+        for m in bunches[0]:
+            transpose_and_quantise([m])
+        sort_words(bunches[1])
         for b in range(len(bunches)):
             half = len(bunches[b]) // 2
             for m in bunches[b][:half]:
                 multiply(m)
             if b + 1 < len(bunches):
-                for m in bunches[b + 1]:
-                    transpose_and_quantise(m)
+                transpose_and_quantise(bunches[b + 1])
+            if b + 2 < len(bunches):
+                sort_words(bunches[b + 2])
             for m in bunches[b][half:]:
                 multiply(m)

@@ -60,6 +60,7 @@ def tile_linear_pa_e_kernel(tc, x, weights_words, weights_scales, path_weights, 
 
         words_i32 = weights_words.bitcast(I32)
         scales_i32 = weights_scales.bitcast(I32)
+        scales_f32 = weights_scales.bitcast(F32)
 
         def load_x(first_row, n_rows):
             rows = slice(first_row, first_row + n_rows)
@@ -69,10 +70,16 @@ def tile_linear_pa_e_kernel(tc, x, weights_words, weights_scales, path_weights, 
             groups = slice(PASSES * l, PASSES * (l + 1))
             nc.vector.memset(w_planes[l][:].bitcast(I32), 0)
             for r in range(4):
-                nc.sync.dma_start(
-                    out=w_planes[l][r:P:32, :, :].bitcast(I32),
-                    in_=scales_i32[groups, r:16:4, :].rearrange("g q n -> q g n"),
-                )
+                if l == DEGREES - 1:
+                    nc.sync.dma_start(
+                        out=w_planes[l][r:P:32, :, :].bitcast(I32),
+                        in_=scales_i32[groups, r:16:4, :].rearrange("g q n -> q g n"),
+                    )
+                else:
+                    nc.gpsimd.dma_start(
+                        out=w_planes[l][r:P:32, :, :].bitcast(F32),
+                        in_=scales_f32[groups, r:16:4, :].rearrange("g q n -> q g n"),
+                    )
             nc.sync.dma_start(
                 out=w_words[l][:].bitcast(I32),
                 in_=words_i32[groups, :, :].rearrange("g p w -> p g w"),

@@ -60,7 +60,6 @@ def tile_linear_pa_e_kernel(tc, x, weights_words, weights_scales, path_weights, 
 
         words_i32 = weights_words.bitcast(I32)
         scales_i32 = weights_scales.bitcast(I32)
-        scales_f32 = weights_scales.bitcast(F32)
 
         def load_x(first_row, n_rows):
             rows = slice(first_row, first_row + n_rows)
@@ -70,26 +69,19 @@ def tile_linear_pa_e_kernel(tc, x, weights_words, weights_scales, path_weights, 
             groups = slice(PASSES * l, PASSES * (l + 1))
             nc.vector.memset(w_planes[l][:].bitcast(I32), 0)
             for r in range(4):
-                if l == DEGREES - 1:
-                    nc.sync.dma_start(
-                        out=w_planes[l][r:P:32, :, :].bitcast(I32),
-                        in_=scales_i32[groups, r:16:4, :].rearrange("g q n -> q g n"),
-                    )
-                else:
-                    nc.gpsimd.dma_start(
-                        out=w_planes[l][r:P:32, :, :].bitcast(F32),
-                        in_=scales_f32[groups, r:16:4, :].rearrange("g q n -> q g n"),
-                    )
+                nc.sync.dma_start(
+                    out=w_planes[l][r:P:32, :, :].bitcast(I32),
+                    in_=scales_i32[groups, r:16:4, :].rearrange("g q n -> q g n"),
+                )
             nc.sync.dma_start(
                 out=w_words[l][:].bitcast(I32),
                 in_=words_i32[groups, :, :].rearrange("g p w -> p g w"),
             )
 
-        def sort_words(rows):
-            block = slice(rows[-1], rows[0] + 1)
+        def sort_words(m):
             nc.vector.tensor_copy(
-                out=x_sorted[:, block, :].bitcast(F32).rearrange("p m (g u q) -> p (m g) u q", g=PASSES, u=WORDS),
-                in_=x_sb[:, block, :].bitcast(F32).rearrange("p m (g q u) -> p (m g) u q", g=PASSES, u=WORDS),
+                out=x_sorted[:, m, :].bitcast(F32).rearrange("p (g u q) -> p g u q", g=PASSES, u=WORDS),
+                in_=x_sb[:, m, :].bitcast(F32).rearrange("p (g q u) -> p g u q", g=PASSES, u=WORDS),
             )
 
         def quantise(m):
@@ -106,15 +98,16 @@ def tile_linear_pa_e_kernel(tc, x, weights_words, weights_scales, path_weights, 
                 xt = xt_pool.tile([P, PASSES * WORDS, P], F32)
                 for j in range(PASSES * WORDS):
                     nc.tensor.transpose(xt[:, j, :], x_words[:, P * j : P * (j + 1)], ident[:])
-                nc.vector.tensor_copy(
-                    out=grouped[:, m, :].bitcast(F32).rearrange("p (g n u) -> p g n u", g=PASSES, u=WORDS),
-                    in_=xt[:].rearrange("p (g u) n -> p g n u", u=WORDS),
-                )
+                pairs = grouped[:, m, :].bitcast(F32).rearrange("p (g n u) -> p g n u", g=PASSES, u=WORDS)
+                if m % 2 == 1:
+                    nc.scalar.copy(out=pairs, in_=xt[:].rearrange("p (g u) n -> p g n u", u=WORDS))
+                else:
+                    nc.vector.tensor_copy(out=pairs, in_=xt[:].rearrange("p (g u) n -> p g n u", u=WORDS))
                 if i > 0:
                     quantise(rows[i - 1])
             quantise(rows[-1])
 
-        def multiply(m):
+        def multiply(m, on_vector):
             l = DEGREE_OF_ROW[m]
             for h in range(HALVES):
                 acc = acc_pool.tile([P, N_TILE], F32)
@@ -129,12 +122,15 @@ def tile_linear_pa_e_kernel(tc, x, weights_words, weights_scales, path_weights, 
                         stop=(g == PASSES - 1),
                     )
                 result = out_sb[:, m, N_TILE * h : N_TILE * (h + 1)]
-                nc.scalar.activation(
-                    out=result,
-                    in_=acc[:],
-                    func=mybir.ActivationFunctionType.Copy,
-                    scale=factor[:, l : l + 1],
-                )
+                if on_vector:
+                    nc.vector.tensor_scalar_mul(out=result, in0=acc[:], scalar1=factor[:, l : l + 1])
+                else:
+                    nc.scalar.activation(
+                        out=result,
+                        in_=acc[:],
+                        func=mybir.ActivationFunctionType.Copy,
+                        scale=factor[:, l : l + 1],
+                    )
                 if m < STORE_ROWS:
                     nc.sync.dma_start(out=out[:, m, N_TILE * h : N_TILE * (h + 1)], in_=result)
             if m >= STORE_ROWS and m % STORE_ROWS == 0:
@@ -146,7 +142,11 @@ def tile_linear_pa_e_kernel(tc, x, weights_words, weights_scales, path_weights, 
 
         loaded = set()
         for rows in bunches:
-            load_x(rows[-1], len(rows))
+            if rows == bunches[0]:
+                for m in rows:
+                    load_x(m, 1)
+            else:
+                load_x(rows[-1], len(rows))
             for m in rows:
                 if DEGREE_OF_ROW[m] not in loaded:
                     loaded.add(DEGREE_OF_ROW[m])
@@ -154,17 +154,19 @@ def tile_linear_pa_e_kernel(tc, x, weights_words, weights_scales, path_weights, 
         nc.vector.tensor_copy(out=factor[:], in_=factor_bf[:])
 
         for m in bunches[0]:
-            sort_words([m])
+            sort_words(m)
         for m in bunches[0]:
             transpose_and_quantise([m])
-        sort_words(bunches[1])
+        for m in bunches[1]:
+            sort_words(m)
         for b in range(len(bunches)):
             half = len(bunches[b]) // 2
             for m in bunches[b][:half]:
-                multiply(m)
+                multiply(m, on_vector=(m == bunches[b][half - 1]))
             if b + 1 < len(bunches):
                 transpose_and_quantise(bunches[b + 1])
             if b + 2 < len(bunches):
-                sort_words(bunches[b + 2])
+                for m in bunches[b + 2]:
+                    sort_words(m)
             for m in bunches[b][half:]:
-                multiply(m)
+                multiply(m, on_vector=False)

@@ -51,12 +51,15 @@ def tile_linear_pa_e_kernel(tc, x, weights_words, weights_scales, path_weights, 
         x_planes = keep.tile([P, ROWS, PASSES, P], U8, align_bytes=64)
         out_sb = keep.tile([P, ROWS, COUT], F32)
         ident = keep.tile([P, P], F32)
-        factor_bf = keep.tile([P, DEGREES], BF16)
+        factor_row = keep.tile([P, DEGREES], BF16)
+        ones = keep.tile([P, P], BF16)
         factor = keep.tile([P, DEGREES], F32)
 
         masks.make_identity(nc, ident[:])
 
-        nc.scalar.dma_start(out=factor_bf[:], in_=path_weights.partition_broadcast(P))
+        nc.vector.memset(factor_row[:], 0.0)
+        nc.vector.memset(ones[:], 1.0)
+        nc.scalar.dma_start(out=factor_row[0:1, :], in_=path_weights.rearrange("(o d) -> o d", o=1))
 
         words_i32 = weights_words.bitcast(I32)
         scales_i32 = weights_scales.bitcast(I32)
@@ -151,12 +154,14 @@ def tile_linear_pa_e_kernel(tc, x, weights_words, weights_scales, path_weights, 
                 if DEGREE_OF_ROW[m] not in loaded:
                     loaded.add(DEGREE_OF_ROW[m])
                     load_weight(DEGREE_OF_ROW[m])
-        nc.vector.tensor_copy(out=factor[:], in_=factor_bf[:])
 
         for m in bunches[0]:
             sort_words(m)
         for m in bunches[0]:
             transpose_and_quantise([m])
+        acc = acc_pool.tile([P, N_TILE], F32)
+        nc.tensor.matmul(out=acc[:, 0:DEGREES], lhsT=ones[:], rhs=factor_row[:], start=True, stop=True)
+        nc.vector.tensor_copy(out=factor[:], in_=acc[:, 0:DEGREES])
         for m in bunches[1]:
             sort_words(m)
         for b in range(len(bunches)):

@@ -23,7 +23,7 @@ HALVES = COUT // N_TILE
 WORDS = 2
 BUNCH = 4
 HEAD = 2
-STORE_ROWS = 2
+STORE_GROUPS = [4, 4, 2, 2, 1, 1]
 
 DEGREE_OF_ROW = [l for l in range(DEGREES) for i in range(2 * l + 1)]
 
@@ -110,6 +110,10 @@ def tile_linear_pa_e_kernel(tc, x, weights_words, weights_scales, path_weights, 
                     quantise(rows[i - 1])
             quantise(rows[-1])
 
+        rows_of_store = {}
+        for i in range(len(STORE_GROUPS)):
+            rows_of_store[ROWS - sum(STORE_GROUPS[: i + 1])] = STORE_GROUPS[i]
+
         def multiply(m, on_vector):
             l = DEGREE_OF_ROW[m]
             for h in range(HALVES):
@@ -134,10 +138,10 @@ def tile_linear_pa_e_kernel(tc, x, weights_words, weights_scales, path_weights, 
                         func=mybir.ActivationFunctionType.Copy,
                         scale=factor[:, l : l + 1],
                     )
-                if m < STORE_ROWS:
+                if m < ROWS - sum(STORE_GROUPS):
                     nc.sync.dma_start(out=out[:, m, N_TILE * h : N_TILE * (h + 1)], in_=result)
-            if m >= STORE_ROWS and m % STORE_ROWS == 0:
-                rows = slice(m, m + STORE_ROWS)
+            if m in rows_of_store:
+                rows = slice(m, m + rows_of_store[m])
                 nc.sync.dma_start(out=out[:, rows, :], in_=out_sb[:, rows, :])
 
         order = list(range(ROWS - 1, -1, -1))

@@ -24,6 +24,7 @@ WORDS = 2
 BUNCH = 4
 HEAD = 2
 STORE_GROUPS = [4, 4, 2, 2, 1, 1]
+PLANES_BEHIND_STORE = {12: 1, 8: 0}
 
 DEGREE_OF_ROW = [l for l in range(DEGREES) for i in range(2 * l + 1)]
 
@@ -68,14 +69,16 @@ def tile_linear_pa_e_kernel(tc, x, weights_words, weights_scales, path_weights, 
             rows = slice(first_row, first_row + n_rows)
             nc.sync.dma_start(out=x_sb[:, rows, :], in_=x[:, rows, :])
 
-        def load_weight(l):
+        def load_planes(l):
             groups = slice(PASSES * l, PASSES * (l + 1))
-            nc.vector.memset(w_planes[l][:].bitcast(I32), 0)
             for r in range(4):
                 nc.sync.dma_start(
                     out=w_planes[l][r:P:32, :, :].bitcast(I32),
                     in_=scales_i32[groups, r:16:4, :].rearrange("g q n -> q g n"),
                 )
+
+        def load_words(l):
+            groups = slice(PASSES * l, PASSES * (l + 1))
             nc.sync.dma_start(
                 out=w_words[l][:].bitcast(I32),
                 in_=words_i32[groups, :, :].rearrange("g p w -> p g w"),
@@ -143,6 +146,8 @@ def tile_linear_pa_e_kernel(tc, x, weights_words, weights_scales, path_weights, 
             if m in rows_of_store:
                 rows = slice(m, m + rows_of_store[m])
                 nc.sync.dma_start(out=out[:, rows, :], in_=out_sb[:, rows, :])
+            if m in PLANES_BEHIND_STORE:
+                load_planes(PLANES_BEHIND_STORE[m])
 
         order = list(range(ROWS - 1, -1, -1))
         bunches = [order[:HEAD]] + [order[i : i + BUNCH] for i in range(HEAD, ROWS, BUNCH)]
@@ -155,9 +160,14 @@ def tile_linear_pa_e_kernel(tc, x, weights_words, weights_scales, path_weights, 
             else:
                 load_x(rows[-1], len(rows))
             for m in rows:
-                if DEGREE_OF_ROW[m] not in loaded:
-                    loaded.add(DEGREE_OF_ROW[m])
-                    load_weight(DEGREE_OF_ROW[m])
+                l = DEGREE_OF_ROW[m]
+                if l not in loaded:
+                    loaded.add(l)
+                    nc.vector.memset(w_planes[l][:].bitcast(I32), 0)
+                    if l == DEGREES - 1:
+                        load_planes(l)
+                    load_words(l)
+        load_planes(DEGREES - 2)
 
         for m in bunches[0]:
             sort_words(m)

@@ -132,7 +132,7 @@ def tile_linear_pa_e_kernel(tc, x, weights_words, weights_scales, path_weights, 
                         stop=(g == PASSES - 1),
                     )
                 result = out_sb[:, m, N_TILE * h : N_TILE * (h + 1)]
-                if on_vector:
+                if on_vector and h == 0:
                     nc.vector.tensor_scalar_mul(out=result, in0=acc[:], scalar1=factor[:, l : l + 1])
                 else:
                     nc.scalar.activation(

@@ -56,11 +56,11 @@ def tile_linear_pa_e_kernel(tc, x, weights_words, weights_scales, path_weights, 
         ones = keep.tile([P, P], BF16)
         factor = keep.tile([P, DEGREES], F32)
 
-        masks.make_identity(nc, ident[:])
-
-        nc.vector.memset(factor_row[:], 0.0)
-        nc.vector.memset(ones[:], 1.0)
+        nc.gpsimd.memset(factor_row[:], 0.0)
+        nc.gpsimd.memset(ones[:], 1.0)
         nc.scalar.dma_start(out=factor_row[0:1, :], in_=path_weights.rearrange("(o d) -> o d", o=1))
+
+        masks.make_identity(nc, ident[:])
 
         words_i32 = weights_words.bitcast(I32)
         scales_i32 = weights_scales.bitcast(I32)
@@ -164,9 +164,9 @@ def tile_linear_pa_e_kernel(tc, x, weights_words, weights_scales, path_weights, 
                 if l not in loaded:
                     loaded.add(l)
                     nc.vector.memset(w_planes[l][:].bitcast(I32), 0)
+                    load_words(l)
                     if l == DEGREES - 1:
                         load_planes(l)
-                    load_words(l)
         load_planes(DEGREES - 2)
 
         for m in bunches[0]:

from contextlib import ExitStack

import concourse.masks as masks
import concourse.mybir as mybir

F32 = mybir.dt.float32
BF16 = mybir.dt.bfloat16
I32 = mybir.dt.int32
U32 = mybir.dt.uint32
U8 = mybir.dt.uint8
FP8X4 = mybir.dt.float8_e4m3fn_x4
FP4X4 = mybir.dt.float4_e2m1fn_x4

P = 128
ROWS = 16
DEGREES = 4
CIN = 1024
COUT = 1024
K_PASS = 4 * P
PASSES = CIN // K_PASS
N_TILE = 512
HALVES = COUT // N_TILE
WORDS = 2
BUNCH = 4
HEAD = 2
STORE_GROUPS = [4, 4, 2, 2, 1, 1]
PLANES_BEHIND_STORE = {12: 1, 8: 0}

DEGREE_OF_ROW = [l for l in range(DEGREES) for i in range(2 * l + 1)]

FLOPS = 2 * P * ROWS * CIN * COUT


def tile_linear_pa_e_kernel(tc, x, weights_words, weights_scales, path_weights, out):
    nc = tc.nc
    with ExitStack() as ctx:
        keep = ctx.enter_context(tc.tile_pool(name="keep", bufs=1))
        xt_pool = ctx.enter_context(tc.psum_pool(name="xt_pool", bufs=BUNCH))
        acc_pool = ctx.enter_context(tc.psum_pool(name="acc_pool", bufs=8 - BUNCH))
        ctx.enter_context(tc.manual_schedule())

        x_sb = keep.tile([P, ROWS, CIN], BF16)
        x_sorted = keep.tile([P, ROWS, CIN], BF16)
        w_words = [
            keep.tile([P, PASSES, 2 * COUT], U8, align_bytes=64, name="w_words%d" % l) for l in range(DEGREES)
        ]
        w_planes = [
            keep.tile([P, PASSES, COUT], U8, align_bytes=64, name="w_planes%d" % l) for l in range(DEGREES)
        ]
        grouped = keep.tile([P, ROWS, CIN], BF16, align_bytes=64)
        x_codes = keep.tile([P, ROWS, PASSES, P], U32, align_bytes=64)
        x_planes = keep.tile([P, ROWS, PASSES, P], U8, align_bytes=64)
        out_sb = keep.tile([P, ROWS, COUT], F32)
        ident = keep.tile([P, P], F32)
        factor_row = keep.tile([P, DEGREES], BF16)
        ones = keep.tile([P, P], BF16)
        factor = keep.tile([P, DEGREES], F32)

        nc.gpsimd.memset(factor_row[:], 0.0)
        nc.gpsimd.memset(ones[:], 1.0)
        nc.scalar.dma_start(out=factor_row[0:1, :], in_=path_weights.rearrange("(o d) -> o d", o=1))

        masks.make_identity(nc, ident[:])

        words_i32 = weights_words.bitcast(I32)
        scales_i32 = weights_scales.bitcast(I32)

        def load_x(first_row, n_rows):
            rows = slice(first_row, first_row + n_rows)
            nc.sync.dma_start(out=x_sb[:, rows, :], in_=x[:, rows, :])

        def load_planes(l):
            groups = slice(PASSES * l, PASSES * (l + 1))
            for r in range(4):
                nc.sync.dma_start(
                    out=w_planes[l][r:P:32, :, :].bitcast(I32),
                    in_=scales_i32[groups, r:16:4, :].rearrange("g q n -> q g n"),
                )

        def load_words(l):
            groups = slice(PASSES * l, PASSES * (l + 1))
            nc.sync.dma_start(
                out=w_words[l][:].bitcast(I32),
                in_=words_i32[groups, :, :].rearrange("g p w -> p g w"),
            )

        def sort_words(m):
            nc.vector.tensor_copy(
                out=x_sorted[:, m, :].bitcast(F32).rearrange("p (g u q) -> p g u q", g=PASSES, u=WORDS),
                in_=x_sb[:, m, :].bitcast(F32).rearrange("p (g q u) -> p g u q", g=PASSES, u=WORDS),
            )

        def quantise(m):
            nc.vector.quantize_mx(
                out=x_codes[:, m, :, :].rearrange("p g n -> p (g n)").bitcast(FP8X4),
                scales=x_planes[:, m, :, :].rearrange("p g n -> p (g n)"),
                in_=grouped[:, m, :],
            )

        def transpose_and_quantise(rows):
            for i in range(len(rows)):
                m = rows[i]
                x_words = x_sorted[:, m, :].bitcast(F32)
                xt = xt_pool.tile([P, PASSES * WORDS, P], F32)
                for j in range(PASSES * WORDS):
                    nc.tensor.transpose(xt[:, j, :], x_words[:, P * j : P * (j + 1)], ident[:])
                pairs = grouped[:, m, :].bitcast(F32).rearrange("p (g n u) -> p g n u", g=PASSES, u=WORDS)
                if m % 2 == 1:
                    nc.scalar.copy(out=pairs, in_=xt[:].rearrange("p (g u) n -> p g n u", u=WORDS))
                else:
                    nc.vector.tensor_copy(out=pairs, in_=xt[:].rearrange("p (g u) n -> p g n u", u=WORDS))
                if i > 0:
                    quantise(rows[i - 1])
            quantise(rows[-1])

        rows_of_store = {}
        for i in range(len(STORE_GROUPS)):
            rows_of_store[ROWS - sum(STORE_GROUPS[: i + 1])] = STORE_GROUPS[i]

        def multiply(m, on_vector):
            l = DEGREE_OF_ROW[m]
            for h in range(HALVES):
                acc = acc_pool.tile([P, N_TILE], F32)
                for g in range(PASSES):
                    nc.tensor.matmul_mx(
                        out=acc[:],
                        lhsT=x_codes[:, m, g, :].bitcast(FP8X4),
                        lhsT_scale=x_planes[:, m, g, :],
                        rhs=w_words[l][:, g, 2 * N_TILE * h : 2 * N_TILE * (h + 1)].bitcast(FP4X4),
                        rhs_scale=w_planes[l][:, g, N_TILE * h : N_TILE * (h + 1)],
                        start=(g == 0),
                        stop=(g == PASSES - 1),
                    )
                result = out_sb[:, m, N_TILE * h : N_TILE * (h + 1)]
                if on_vector and h == 0:
                    nc.vector.tensor_scalar_mul(out=result, in0=acc[:], scalar1=factor[:, l : l + 1])
                else:
                    nc.scalar.activation(
                        out=result,
                        in_=acc[:],
                        func=mybir.ActivationFunctionType.Copy,
                        scale=factor[:, l : l + 1],
                    )
                if m < ROWS - sum(STORE_GROUPS):
                    nc.sync.dma_start(out=out[:, m, N_TILE * h : N_TILE * (h + 1)], in_=result)
            if m in rows_of_store:
                rows = slice(m, m + rows_of_store[m])
                nc.sync.dma_start(out=out[:, rows, :], in_=out_sb[:, rows, :])
            if m in PLANES_BEHIND_STORE:
                load_planes(PLANES_BEHIND_STORE[m])

        order = list(range(ROWS - 1, -1, -1))
        bunches = [order[:HEAD]] + [order[i : i + BUNCH] for i in range(HEAD, ROWS, BUNCH)]

        loaded = set()
        for rows in bunches:
            if rows == bunches[0]:
                for m in rows:
                    load_x(m, 1)
            else:
                load_x(rows[-1], len(rows))
            for m in rows:
                l = DEGREE_OF_ROW[m]
                if l not in loaded:
                    loaded.add(l)
                    nc.vector.memset(w_planes[l][:].bitcast(I32), 0)
                    load_words(l)
                    if l == DEGREES - 1:
                        load_planes(l)
        load_planes(DEGREES - 2)

        for m in bunches[0]:
            sort_words(m)
        for m in bunches[0]:
            transpose_and_quantise([m])
        acc = acc_pool.tile([P, N_TILE], F32)
        nc.tensor.matmul(out=acc[:, 0:DEGREES], lhsT=ones[:], rhs=factor_row[:], start=True, stop=True)
        nc.vector.tensor_copy(out=factor[:], in_=acc[:, 0:DEGREES])
        for m in bunches[1]:
            sort_words(m)
        for b in range(len(bunches)):
            half = len(bunches[b]) // 2
            for m in bunches[b][:half]:
                multiply(m, on_vector=(m == bunches[b][half - 1]))
            if b + 1 < len(bunches):
                transpose_and_quantise(bunches[b + 1])
            if b + 2 < len(bunches):
                for m in bunches[b + 2]:
                    sort_words(m)
            for m in bunches[b][half:]:
                multiply(m, on_vector=False)
